import numpy as np
import ml_dtypes


def mxq(x, axis, fmt="e4m3"):
    dtype, down = {"e4m3": (ml_dtypes.float8_e4m3fn, 7), "e5m2": (ml_dtypes.float8_e5m2, 14)}[fmt]
    v = np.moveaxis(np.asarray(x, np.float32).astype(ml_dtypes.bfloat16).astype(np.float64), axis, -1)
    blocks = v.reshape(v.shape[:-1] + (-1, 32))
    amax = np.abs(blocks).max(-1, keepdims=True)
    byte = np.maximum(np.where(amax > 0, np.frexp(amax)[1] - 1 + 127, 0) - down, 1)
    scale = np.exp2(byte - 127.0)
    codes = (blocks / scale).astype(np.float32).astype(dtype).astype(np.float64)
    return np.moveaxis((codes * scale).reshape(v.shape), -1, axis)


WIDE = False


def mx_kscale(k):
    if not WIDE:
        return np.ones(k)
    levels = np.array([10, -10, 5, -5, 0])
    if k % 512:
        return np.exp2(np.random.permutation(np.resize(levels, k // 32))).repeat(32)
    a = np.empty((k // 512, 16))
    for p in range(k // 512):
        a[p, :8] = np.random.permutation(np.resize(levels, 8))
        for g in range(8):
            far = levels[np.abs(levels - a[p, g]) >= 10]
            a[p, g + 8] = far[np.random.randint(len(far))]
    return np.exp2(a.ravel()).repeat(32)


BF16 = ml_dtypes.bfloat16


def bf(x):
    return np.asarray(x, np.float32).astype(BF16)


def f64(x):
    return np.asarray(x).astype(np.float64)


B, K, N = 2048, 512, 1024
NACT = 4


def act_deriv(y):
    rows, cols = y.shape
    y3 = y.reshape(rows, cols // NACT, NACT)
    c3 = np.cos(y3[..., 3])
    d = np.stack(
        [np.ones_like(y3[..., 0]),
         -np.sin(y3[..., 1]),
         np.cos(y3[..., 2]),
         1.0 / (c3 * c3)],
        axis=-1,
    )
    return d.reshape(rows, cols)


def setup_inputs():
    s = mx_kscale(B)[:, None]
    u = mx_kscale(N)
    h = np.tile(np.array([1.0, 1.0, 1.0, 0.5]), N // NACT)
    x0 = bf(np.random.standard_normal((B, K)))
    w0 = bf(np.random.uniform(-1.0, 1.0, (N, K)) / np.sqrt(K) * h[:, None])
    g = bf(np.random.standard_normal((B, N)) * np.exp2(np.random.randint(-6, 1, (B, 1))) * 2.0 / s * u[None, :])
    y = f64(x0) @ f64(w0).T
    return {"x": bf(f64(x0) * s), "weight": bf(f64(w0) / u[:, None]), "y": np.asarray(y, np.float32), "grad_out": g}


def reference(x, weight, y, grad_out):
    dy = f64(grad_out) * act_deriv(f64(y))
    dx = mxq(dy, 1, "e5m2") @ mxq(f64(weight), 0, "e4m3")
    dw = mxq(dy, 0, "e5m2").T @ mxq(f64(x), 0, "e4m3")
    return dx, dw

@@ -1,0 +1,314 @@
+from contextlib import ExitStack
+import math
+
+import concourse.mybir as mybir
+from concourse.masks import make_identity
+
+TOKENS, IN_F, OUT_F = 2048, 512, 1024
+FLOPS = 2 * 2 * TOKENS * IN_F * OUT_F
+BYTES = TOKENS * IN_F * 2 + OUT_F * IN_F * 2 + TOKENS * (OUT_F * 3 // 4) * 4 + TOKENS * OUT_F * 2 + (TOKENS + OUT_F) * IN_F * 4
+
+F32 = mybir.dt.float32
+I32 = mybir.dt.int32
+BF16 = mybir.dt.bfloat16
+U32 = mybir.dt.uint32
+U8 = mybir.dt.uint8
+E4 = mybir.dt.float8_e4m3fn_x4
+E5 = mybir.dt.float8_e5m2_x4
+ACT = mybir.ActivationFunctionType
+ALU = mybir.AluOpType
+
+P = 128
+PACK = 4
+PASS = P * PACK
+HALF_PI = math.pi / 2.0
+
+
+def tile_mylayerfunc_v_kernel(tc, x, weight, y, grad_out, out_0, out_1):
+    nc = tc.nc
+    n_tok = TOKENS // PASS
+    n_col = OUT_F // PASS
+    n_chunks = n_tok * n_col
+
+    with ExitStack() as ctx:
+        consts = ctx.enter_context(tc.tile_pool(name="consts", bufs=1))
+        ypool = ctx.enter_context(tc.tile_pool(name="ypool", bufs=5))
+        gpool = ctx.enter_context(tc.tile_pool(name="gpool", bufs=6))
+        rawp = ctx.enter_context(tc.tile_pool(name="rawp", bufs=3))
+        dpool = ctx.enter_context(tc.tile_pool(name="dpool", bufs=6))
+        stage = ctx.enter_context(tc.tile_pool(name="stage", bufs=2))
+        keep = ctx.enter_context(tc.tile_pool(name="keep", bufs=1))
+        acodes = ctx.enter_context(tc.tile_pool(name="acodes", bufs=3))
+        outp = ctx.enter_context(tc.tile_pool(name="outp", bufs=2))
+        accp = ctx.enter_context(tc.psum_pool(name="accp", bufs=1))
+        tpp = ctx.enter_context(tc.psum_pool(name="tpp", bufs=2))
+        dxp = ctx.enter_context(tc.psum_pool(name="dxp", bufs=2))
+        ctx.enter_context(tc.manual_schedule())
+
+        ident = consts.tile([P, P], F32, name="ident")
+        make_identity(nc, ident[:])
+        warm = consts.tile([P, 1], F32, name="warm")
+        nc.vector.memset(warm[:], 0.0)
+        nc.scalar.activation(out=warm[:], in_=warm[:], func=ACT.Sin)
+
+        y_t = {}
+        g_t = {}
+        d_t = {}
+        raw_t = {}
+        e4_grouped = {}
+        e4_q = {}
+        a_q = {}
+        b_q = {}
+        acc = {}
+        grouped_a = {}
+        grouped_b = {}
+        tp_t = {}
+
+        def rows_of(i):
+            return slice(i * PASS, (i + 1) * PASS)
+
+        def load_y(n):
+            col, tok = divmod(n, n_tok)
+            yt = ypool.tile([P, PACK, PASS], F32, name="yt")
+            nc.sync.dma_start(out=yt[:], in_=y[rows_of(tok), rows_of(col)].rearrange("(p j) n -> p j n", j=PACK))
+            y_t[n] = yt
+
+        def load_g(n):
+            col, tok = divmod(n, n_tok)
+            gt = gpool.tile([P, PACK, PASS], BF16, name="gt", align_bytes=64)
+            nc.sync.dma_start(out=gt[:], in_=grad_out[rows_of(tok), rows_of(col)].rearrange("(p j) n -> p j n", j=PACK))
+            g_t[n] = gt
+
+        def load_e4(label, src, i):
+            raw = rawp.tile([P, PACK, IN_F], BF16, name="raw")
+            nc.sync.dma_start(out=raw[:], in_=src[rows_of(i), :].rearrange("(p j) k -> p j k", j=PACK))
+            raw_t[label] = raw
+
+        def interleave_e4(label):
+            grouped = stage.tile([P, IN_F, PACK], BF16, name="grouped_e4", align_bytes=64)
+            nc.vector.tensor_copy(out=grouped[:], in_=raw_t[label][:].rearrange("p j k -> p k j"))
+            e4_grouped[label] = grouped
+
+        def quantize_e4(label):
+            codes = keep.tile([P, IN_F], U32, name="codes_%s" % label, align_bytes=64)
+            scales = keep.tile([P, IN_F], U8, name="scales_%s" % label, align_bytes=64)
+            nc.vector.quantize_mx(out=codes[:].bitcast(E4), scales=scales[:], in_=e4_grouped[label][:].rearrange("p k j -> p (k j)"))
+            e4_q[label] = (codes, scales)
+
+        def absy(n):
+            d = dpool.tile([P, 3, PACK, P], F32, name="d")
+            yi = y_t[n][:].bitcast(I32).rearrange("p j (q m) -> p m j q", m=4)
+            nc.vector.tensor_scalar(out=d[:, 1:3, :, :].bitcast(I32), in0=yi[:, 2:4, :, :], scalar1=0x7FFFFFFF, scalar2=None, op0=ALU.bitwise_and)
+            d_t[n] = d
+
+        def trig(n):
+            yc = y_t[n][:].rearrange("p j (q m) -> p j q m", m=4)
+            d = d_t[n]
+            nc.scalar.activation(out=d[:, 2, :, :], in_=d[:, 2, :, :], func=ACT.Sin, scale=-2.0, bias=HALF_PI)
+            nc.scalar.activation(out=d[:, 2, :, :], in_=d[:, 2, :, :], func=ACT.Square, scale=0.5, bias=0.5)
+            nc.scalar.activation(out=d[:, 1, :, :], in_=d[:, 1, :, :], func=ACT.Sin, scale=-1.0, bias=HALF_PI)
+            nc.scalar.activation(out=d[:, 0, :, :], in_=yc[:, :, :, 1], func=ACT.Sin, scale=-1.0)
+
+        def rsq(n):
+            d = d_t[n]
+            nc.scalar.activation(out=d[:, 2, :, :], in_=d[:, 2, :, :], func=ACT.Abs_reciprocal_sqrt)
+
+        def mult(n):
+            gv = g_t[n][:].rearrange("p j (q m) -> p (j q) m", m=4)
+            nc.vector.tensor_tensor(out=gv[:, :, 1:4], in0=gv[:, :, 1:4], in1=d_t[n][:].rearrange("p m j q -> p (j q) m"), op=ALU.mult)
+
+        def ia(n):
+            ga = stage.tile([P, PASS, PACK], BF16, name="ga", align_bytes=64)
+            nc.vector.tensor_copy(out=ga[:], in_=g_t[n][:].rearrange("p j n -> p n j"))
+            grouped_a[n] = ga
+
+        def qa(n):
+            codes = acodes.tile([P, PASS], U32, name="a_codes", align_bytes=64)
+            scales = acodes.tile([P, PASS], U8, name="a_scales", align_bytes=64)
+            nc.vector.quantize_mx(out=codes[:].bitcast(E5), scales=scales[:], in_=grouped_a[n][:].rearrange("p n j -> p (n j)"))
+            a_q[n] = (codes, scales)
+
+        def ma(n):
+            col, tok = divmod(n, n_tok)
+            codes, scales = a_q[n]
+            xc, xs = e4_q["x%d" % tok]
+            for i in range(PASS // P):
+                if tok == 0:
+                    at = accp.tile([P, IN_F], F32, name="acc%d" % i)
+                    acc[i] = at
+                cols = slice(i * P, (i + 1) * P)
+                nc.tensor.matmul_mx(
+                    out=acc[i][:],
+                    lhsT=codes[:, cols].bitcast(E5),
+                    lhsT_scale=scales[:, cols],
+                    rhs=xc[:].bitcast(E4),
+                    rhs_scale=xs[:],
+                    start=(tok == 0),
+                    stop=(tok == n_tok - 1),
+                )
+
+        def tp(n):
+            words = g_t[n][:].rearrange("p j n -> p (j n)").bitcast(F32)
+            banks = []
+            for b in range(2):
+                bank = tpp.tile([P, 2, 2, P], F32, name="bank")
+                for jj in range(2):
+                    j = 2 * b + jj
+                    for u in range(2):
+                        nc.tensor.transpose(bank[:, jj, u, :], words[:, j * 256 + u : (j + 1) * 256 : 2], ident[:])
+                banks.append(bank)
+            tp_t[n] = banks
+
+        def cb(n):
+            gb = stage.tile([P, PACK, P, PACK], BF16, name="gb", align_bytes=64)
+            gbw = gb[:].bitcast(F32)
+            for b in range(2):
+                nc.scalar.copy(out=gbw[:, 2 * b : 2 * b + 2, :, :], in_=tp_t[n][b][:].rearrange("p j u r -> p j r u"))
+            grouped_b[n] = gb
+
+        def qb(n):
+            codes = keep.tile([P, PASS], U32, name="b_codes%d" % n, align_bytes=64)
+            scales = keep.tile([P, PASS], U8, name="b_scales%d" % n, align_bytes=64)
+            nc.vector.quantize_mx(out=codes[:].bitcast(E5), scales=scales[:], in_=grouped_b[n][:].rearrange("p j r t -> p (j r t)"))
+            b_q[n] = (codes, scales)
+
+        def mb_ox(tok, last):
+            dxo = outp.tile([P, PACK, IN_F], F32, name="dxo")
+            dst = out_0[rows_of(tok), :].rearrange("(r j) k -> r j k", j=PACK)
+            for j in range(PACK):
+                ps = dxp.tile([P, IN_F], F32, name="ps")
+                cols = slice(j * P, (j + 1) * P)
+                for col in range(n_col):
+                    codes, scales = b_q[col * n_tok + tok]
+                    wc, ws = e4_q["w%d" % col]
+                    nc.tensor.matmul_mx(
+                        out=ps[:],
+                        lhsT=codes[:, cols].bitcast(E5),
+                        lhsT_scale=scales[:, cols],
+                        rhs=wc[:].bitcast(E4),
+                        rhs_scale=ws[:],
+                        start=(col == 0),
+                        stop=(col == n_col - 1),
+                    )
+                if last and j % 2 == 1:
+                    nc.vector.tensor_copy(out=dxo[:, j, :], in_=ps[:])
+                else:
+                    nc.scalar.copy(out=dxo[:, j, :], in_=ps[:])
+                if last:
+                    nc.sync.dma_start(out=dst[:, j, :], in_=dxo[:, j, :])
+            if not last:
+                nc.sync.dma_start(out=dst, in_=dxo[:])
+
+        def ow(col, last):
+            dwo = outp.tile([P, PASS // P, IN_F], F32, name="dwo", bufs=1)
+            dst = out_1[rows_of(col), :].rearrange("(i p) k -> p i k", p=P)
+            for i in range(PASS // P):
+                if last and i % 2 == 1:
+                    nc.vector.tensor_copy(out=dwo[:, i, :], in_=acc[i][:])
+                else:
+                    nc.scalar.copy(out=dwo[:, i, :], in_=acc[i][:])
+                if last:
+                    nc.sync.dma_start(out=dst[:, i, :], in_=dwo[:, i, :])
+            if not last:
+                nc.sync.dma_start(out=dst, in_=dwo[:])
+
+        load_y(0)
+        load_e4("x0", x, 0)
+        load_y(1)
+        load_e4("x1", x, 1)
+        load_y(2)
+        load_e4("x2", x, 2)
+        load_y(3)
+
+        absy(0)
+        trig(0)
+        interleave_e4("x0")
+        load_e4("x3", x, 3)
+
+        absy(1)
+        trig(1)
+        quantize_e4("x0")
+        interleave_e4("x1")
+        load_e4("w0", weight, 0)
+
+        absy(2)
+        trig(2)
+        quantize_e4("x1")
+        interleave_e4("x2")
+        load_e4("w1", weight, 1)
+        load_g(0)
+        load_y(4)
+        load_g(1)
+        load_y(5)
+
+        absy(3)
+        trig(3)
+        quantize_e4("x2")
+        interleave_e4("x3")
+        load_g(2)
+        load_y(6)
+        load_y(7)
+        load_g(3)
+        load_g(4)
+        load_g(5)
+
+        for n in range(4):
+            rsq(n)
+
+        interleave_e4("w0")
+        quantize_e4("x3")
+        interleave_e4("w1")
+        quantize_e4("w0")
+
+        mult(0)
+        quantize_e4("w1")
+        absy(4)
+        tp(0)
+        trig(4)
+        cb(0)
+        ia(0)
+        load_g(6)
+
+        for n in range(n_chunks):
+            col, tok = divmod(n, n_tok)
+            last = n == n_chunks - 1
+            if n == 3:
+                qa(n)
+                ma(n)
+                qb(n)
+                ow(0, False)
+                mult(n + 1)
+                tp(n + 1)
+                cb(n + 1)
+                ia(n + 1)
+                continue
+            if not last:
+                mult(n + 1)
+                if n == 0:
+                    absy(5)
+                if n == 1:
+                    absy(6)
+                tp(n + 1)
+                if n < 3:
+                    trig(n + 5)
+                cb(n + 1)
+                if n == 2:
+                    for k in range(4, 8):
+                        rsq(k)
+            if last:
+                qb(n)
+                qa(n)
+                mb_ox(tok, True)
+                ma(n)
+                ow(1, True)
+            else:
+                qa(n)
+                ma(n)
+                if n == 1:
+                    absy(7)
+                qb(n)
+                if col == 1:
+                    mb_ox(tok, False)
+                ia(n + 1)
+                if n == 0:
+                    load_g(7)

@@ -86,7 +86,7 @@ def tile_mylayerfunc_v_kernel(tc, x, weight, y, grad_out, out_0, out_1):
 
         def interleave_e4(label):
             grouped = stage.tile([P, IN_F, PACK], BF16, name="grouped_e4", align_bytes=64)
-            nc.vector.tensor_copy(out=grouped[:], in_=raw_t[label][:].rearrange("p j k -> p k j"))
+            nc.vector.tensor_copy(out=grouped[:].rearrange("p (c i) j -> p c j i", i=4), in_=raw_t[label][:].rearrange("p j (c i) -> p c j i", i=4))
             e4_grouped[label] = grouped
 
         def quantize_e4(label):
@@ -119,7 +119,7 @@ def tile_mylayerfunc_v_kernel(tc, x, weight, y, grad_out, out_0, out_1):
 
         def ia(n):
             ga = stage.tile([P, PASS, PACK], BF16, name="ga", align_bytes=64)
-            nc.vector.tensor_copy(out=ga[:], in_=g_t[n][:].rearrange("p j n -> p n j"))
+            nc.vector.tensor_copy(out=ga[:].rearrange("p (c i) j -> p c j i", i=4), in_=g_t[n][:].rearrange("p j (c i) -> p c j i", i=4))
             grouped_a[n] = ga
 
         def qa(n):

@@ -41,8 +41,7 @@ def tile_mylayerfunc_v_kernel(tc, x, weight, y, grad_out, out_0, out_1):
         acodes = ctx.enter_context(tc.tile_pool(name="acodes", bufs=3))
         outp = ctx.enter_context(tc.tile_pool(name="outp", bufs=2))
         accp = ctx.enter_context(tc.psum_pool(name="accp", bufs=1))
-        tpp = ctx.enter_context(tc.psum_pool(name="tpp", bufs=2))
-        dxp = ctx.enter_context(tc.psum_pool(name="dxp", bufs=2))
+        wkp = ctx.enter_context(tc.psum_pool(name="wkp", bufs=4))
         ctx.enter_context(tc.manual_schedule())
 
         ident = consts.tile([P, P], F32, name="ident")
@@ -86,7 +85,7 @@ def tile_mylayerfunc_v_kernel(tc, x, weight, y, grad_out, out_0, out_1):
 
         def interleave_e4(label):
             grouped = stage.tile([P, IN_F, PACK], BF16, name="grouped_e4", align_bytes=64)
-            nc.vector.tensor_copy(out=grouped[:].rearrange("p (c i) j -> p c j i", i=4), in_=raw_t[label][:].rearrange("p j (c i) -> p c j i", i=4))
+            nc.vector.tensor_copy(out=grouped[:], in_=raw_t[label][:].rearrange("p j k -> p k j"))
             e4_grouped[label] = grouped
 
         def quantize_e4(label):
@@ -101,13 +100,20 @@ def tile_mylayerfunc_v_kernel(tc, x, weight, y, grad_out, out_0, out_1):
             nc.vector.tensor_scalar(out=d[:, 1:3, :, :].bitcast(I32), in0=yi[:, 2:4, :, :], scalar1=0x7FFFFFFF, scalar2=None, op0=ALU.bitwise_and)
             d_t[n] = d
 
-        def trig(n):
-            yc = y_t[n][:].rearrange("p j (q m) -> p j q m", m=4)
+        def trig3(n):
             d = d_t[n]
             nc.scalar.activation(out=d[:, 2, :, :], in_=d[:, 2, :, :], func=ACT.Sin, scale=-2.0, bias=HALF_PI)
             nc.scalar.activation(out=d[:, 2, :, :], in_=d[:, 2, :, :], func=ACT.Square, scale=0.5, bias=0.5)
+
+        def trig12(n):
+            yc = y_t[n][:].rearrange("p j (q m) -> p j q m", m=4)
+            d = d_t[n]
             nc.scalar.activation(out=d[:, 1, :, :], in_=d[:, 1, :, :], func=ACT.Sin, scale=-1.0, bias=HALF_PI)
             nc.scalar.activation(out=d[:, 0, :, :], in_=yc[:, :, :, 1], func=ACT.Sin, scale=-1.0)
+
+        def trig(n):
+            trig3(n)
+            trig12(n)
 
         def rsq(n):
             d = d_t[n]
@@ -119,7 +125,7 @@ def tile_mylayerfunc_v_kernel(tc, x, weight, y, grad_out, out_0, out_1):
 
         def ia(n):
             ga = stage.tile([P, PASS, PACK], BF16, name="ga", align_bytes=64)
-            nc.vector.tensor_copy(out=ga[:].rearrange("p (c i) j -> p c j i", i=4), in_=g_t[n][:].rearrange("p j (c i) -> p c j i", i=4))
+            nc.vector.tensor_copy(out=ga[:], in_=g_t[n][:].rearrange("p j n -> p n j"))
             grouped_a[n] = ga
 
         def qa(n):
@@ -151,7 +157,7 @@ def tile_mylayerfunc_v_kernel(tc, x, weight, y, grad_out, out_0, out_1):
             words = g_t[n][:].rearrange("p j n -> p (j n)").bitcast(F32)
             banks = []
             for b in range(2):
-                bank = tpp.tile([P, 2, 2, P], F32, name="bank")
+                bank = wkp.tile([P, 2, 2, P], F32, name="bank", tag="wk")
                 for jj in range(2):
                     j = 2 * b + jj
                     for u in range(2):
@@ -160,7 +166,7 @@ def tile_mylayerfunc_v_kernel(tc, x, weight, y, grad_out, out_0, out_1):
             tp_t[n] = banks
 
         def cb(n):
-            gb = stage.tile([P, PACK, P, PACK], BF16, name="gb", align_bytes=64)
+            gb = stage.tile([P, PACK, P, PACK], BF16, name="gb", align_bytes=64, bufs=5)
             gbw = gb[:].bitcast(F32)
             for b in range(2):
                 nc.scalar.copy(out=gbw[:, 2 * b : 2 * b + 2, :, :], in_=tp_t[n][b][:].rearrange("p j u r -> p j r u"))
@@ -172,11 +178,11 @@ def tile_mylayerfunc_v_kernel(tc, x, weight, y, grad_out, out_0, out_1):
             nc.vector.quantize_mx(out=codes[:].bitcast(E5), scales=scales[:], in_=grouped_b[n][:].rearrange("p j r t -> p (j r t)"))
             b_q[n] = (codes, scales)
 
-        def mb_ox(tok, last):
+        def mb_ox(tok):
             dxo = outp.tile([P, PACK, IN_F], F32, name="dxo")
             dst = out_0[rows_of(tok), :].rearrange("(r j) k -> r j k", j=PACK)
             for j in range(PACK):
-                ps = dxp.tile([P, IN_F], F32, name="ps")
+                ps = wkp.tile([P, IN_F], F32, name="ps", tag="wk")
                 cols = slice(j * P, (j + 1) * P)
                 for col in range(n_col):
                     codes, scales = b_q[col * n_tok + tok]
@@ -190,14 +196,8 @@ def tile_mylayerfunc_v_kernel(tc, x, weight, y, grad_out, out_0, out_1):
                         start=(col == 0),
                         stop=(col == n_col - 1),
                     )
-                if last and j % 2 == 1:
-                    nc.vector.tensor_copy(out=dxo[:, j, :], in_=ps[:])
-                else:
-                    nc.scalar.copy(out=dxo[:, j, :], in_=ps[:])
-                if last:
-                    nc.sync.dma_start(out=dst[:, j, :], in_=dxo[:, j, :])
-            if not last:
-                nc.sync.dma_start(out=dst, in_=dxo[:])
+                nc.scalar.copy(out=dxo[:, j, :], in_=ps[:])
+                nc.sync.dma_start(out=dst[:, j, :], in_=dxo[:, j, :])
 
         def ow(col, last):
             dwo = outp.tile([P, PASS // P, IN_F], F32, name="dwo", bufs=1)
@@ -242,7 +242,7 @@ def tile_mylayerfunc_v_kernel(tc, x, weight, y, grad_out, out_0, out_1):
         load_y(5)
 
         absy(3)
-        trig(3)
+        trig3(3)
         quantize_e4("x2")
         interleave_e4("x3")
         load_g(2)
@@ -254,14 +254,13 @@ def tile_mylayerfunc_v_kernel(tc, x, weight, y, grad_out, out_0, out_1):
 
         for n in range(4):
             rsq(n)
+        trig12(3)
 
         interleave_e4("w0")
         quantize_e4("x3")
-        interleave_e4("w1")
-        quantize_e4("w0")
 
         mult(0)
-        quantize_e4("w1")
+        quantize_e4("w0")
         absy(4)
         tp(0)
         trig(4)
@@ -269,46 +268,80 @@ def tile_mylayerfunc_v_kernel(tc, x, weight, y, grad_out, out_0, out_1):
         ia(0)
         load_g(6)
 
-        for n in range(n_chunks):
-            col, tok = divmod(n, n_tok)
-            last = n == n_chunks - 1
-            if n == 3:
-                qa(n)
-                ma(n)
-                qb(n)
-                ow(0, False)
-                mult(n + 1)
-                tp(n + 1)
-                cb(n + 1)
-                ia(n + 1)
-                continue
-            if not last:
-                mult(n + 1)
-                if n == 0:
-                    absy(5)
-                if n == 1:
-                    absy(6)
-                tp(n + 1)
-                if n < 3:
-                    trig(n + 5)
-                cb(n + 1)
-                if n == 2:
-                    for k in range(4, 8):
-                        rsq(k)
-            if last:
-                qb(n)
-                qa(n)
-                mb_ox(tok, True)
-                ma(n)
-                ow(1, True)
-            else:
-                qa(n)
-                ma(n)
-                if n == 1:
-                    absy(7)
-                qb(n)
-                if col == 1:
-                    mb_ox(tok, False)
-                ia(n + 1)
-                if n == 0:
-                    load_g(7)
+        mult(1)
+        absy(5)
+        tp(1)
+        trig(5)
+        cb(1)
+        qa(0)
+        ma(0)
+        ia(1)
+        load_g(7)
+
+        mult(2)
+        absy(6)
+        tp(2)
+        trig(6)
+        qa(1)
+        ma(1)
+        absy(7)
+        ia(2)
+
+        mult(3)
+        interleave_e4("w1")
+        tp(3)
+        trig(7)
+        for n in range(4, 8):
+            rsq(n)
+        qa(2)
+        ma(2)
+        qb(0)
+        ia(3)
+
+        quantize_e4("w1")
+        qa(3)
+        ma(3)
+        cb(2)
+        cb(3)
+
+        mult(4)
+        tp(4)
+        cb(4)
+        ow(0, False)
+        qb(1)
+        ia(4)
+
+        mult(5)
+        tp(5)
+        cb(5)
+        qa(4)
+        ma(4)
+        qb(4)
+        mb_ox(0)
+
+        mult(6)
+        tp(6)
+        cb(6)
+        ia(5)
+        qb(5)
+        mb_ox(1)
+        qb(2)
+
+        mult(7)
+        tp(7)
+        cb(7)
+        qa(5)
+        ma(5)
+        qb(6)
+        mb_ox(2)
+        qb(3)
+        ia(6)
+
+        qb(7)
+        mb_ox(3)
+        ia(7)
+        qa(6)
+        ma(6)
+        qa(7)
+        ma(7)
+        ow(1, True)

@@ -96,8 +96,8 @@ def tile_mylayerfunc_v_kernel(tc, x, weight, y, grad_out, out_0, out_1):
 
         def absy(n):
             d = dpool.tile([P, 3, PACK, P], F32, name="d")
-            yi = y_t[n][:].bitcast(I32).rearrange("p j (q m) -> p m j q", m=4)
-            nc.vector.tensor_scalar(out=d[:, 1:3, :, :].bitcast(I32), in0=yi[:, 2:4, :, :], scalar1=0x7FFFFFFF, scalar2=None, op0=ALU.bitwise_and)
+            yi = y_t[n][:].bitcast(I32).rearrange("p j (q m) -> p (j q) m", m=4)
+            nc.vector.tensor_scalar(out=d[:, 1:3, :, :].bitcast(I32).rearrange("p m j q -> p (j q) m"), in0=yi[:, :, 2:4], scalar1=0x7FFFFFFF, scalar2=None, op0=ALU.bitwise_and)
             d_t[n] = d
 
         def trig3(n):

@@ -165,12 +165,19 @@ def tile_mylayerfunc_v_kernel(tc, x, weight, y, grad_out, out_0, out_1):
                 banks.append(bank)
             tp_t[n] = banks
 
-        def cb(n):
-            gb = stage.tile([P, PACK, P, PACK], BF16, name="gb", align_bytes=64, bufs=5)
-            gbw = gb[:].bitcast(F32)
-            for b in range(2):
+        def cb_bank(n, b, on_vector):
+            if b == 0:
+                gb = stage.tile([P, PACK, P, PACK], BF16, name="gb", align_bytes=64, bufs=5)
+                grouped_b[n] = gb
+            gbw = grouped_b[n][:].bitcast(F32)
+            if on_vector:
+                nc.vector.tensor_copy(out=gbw[:, 2 * b : 2 * b + 2, :, :], in_=tp_t[n][b][:].rearrange("p j u r -> p j r u"))
+            else:
                 nc.scalar.copy(out=gbw[:, 2 * b : 2 * b + 2, :, :], in_=tp_t[n][b][:].rearrange("p j u r -> p j r u"))
-            grouped_b[n] = gb
+
+        def cb(n):
+            cb_bank(n, 0, False)
+            cb_bank(n, 1, False)
 
         def qb(n):
             codes = keep.tile([P, PASS], U32, name="b_codes%d" % n, align_bytes=64)
@@ -264,7 +271,7 @@ def tile_mylayerfunc_v_kernel(tc, x, weight, y, grad_out, out_0, out_1):
         absy(4)
         tp(0)
         trig(4)
-        cb(0)
+        cb_bank(0, 0, False)
         ia(0)
         load_g(6)
 
@@ -272,7 +279,8 @@ def tile_mylayerfunc_v_kernel(tc, x, weight, y, grad_out, out_0, out_1):
         absy(5)
         tp(1)
         trig(5)
-        cb(1)
+        cb_bank(0, 1, True)
+        cb_bank(1, 0, False)
         qa(0)
         ma(0)
         ia(1)
@@ -280,6 +288,7 @@ def tile_mylayerfunc_v_kernel(tc, x, weight, y, grad_out, out_0, out_1):
 
         mult(2)
         absy(6)
+        cb_bank(1, 1, True)
         tp(2)
         trig(6)
         qa(1)

from contextlib import ExitStack
import math

import concourse.mybir as mybir
from concourse.masks import make_identity

TOKENS, IN_F, OUT_F = 2048, 512, 1024
FLOPS = 2 * 2 * TOKENS * IN_F * OUT_F
BYTES = TOKENS * IN_F * 2 + OUT_F * IN_F * 2 + TOKENS * (OUT_F * 3 // 4) * 4 + TOKENS * OUT_F * 2 + (TOKENS + OUT_F) * IN_F * 4

F32 = mybir.dt.float32
I32 = mybir.dt.int32
BF16 = mybir.dt.bfloat16
U32 = mybir.dt.uint32
U8 = mybir.dt.uint8
E4 = mybir.dt.float8_e4m3fn_x4
E5 = mybir.dt.float8_e5m2_x4
ACT = mybir.ActivationFunctionType
ALU = mybir.AluOpType

P = 128
PACK = 4
PASS = P * PACK
HALF_PI = math.pi / 2.0


def tile_mylayerfunc_v_kernel(tc, x, weight, y, grad_out, out_0, out_1):
    nc = tc.nc
    n_tok = TOKENS // PASS
    n_col = OUT_F // PASS
    n_chunks = n_tok * n_col

    with ExitStack() as ctx:
        consts = ctx.enter_context(tc.tile_pool(name="consts", bufs=1))
        ypool = ctx.enter_context(tc.tile_pool(name="ypool", bufs=5))
        gpool = ctx.enter_context(tc.tile_pool(name="gpool", bufs=6))
        rawp = ctx.enter_context(tc.tile_pool(name="rawp", bufs=3))
        dpool = ctx.enter_context(tc.tile_pool(name="dpool", bufs=6))
        stage = ctx.enter_context(tc.tile_pool(name="stage", bufs=2))
        keep = ctx.enter_context(tc.tile_pool(name="keep", bufs=1))
        acodes = ctx.enter_context(tc.tile_pool(name="acodes", bufs=3))
        outp = ctx.enter_context(tc.tile_pool(name="outp", bufs=2))
        accp = ctx.enter_context(tc.psum_pool(name="accp", bufs=1))
        wkp = ctx.enter_context(tc.psum_pool(name="wkp", bufs=4))
        ctx.enter_context(tc.manual_schedule())

        ident = consts.tile([P, P], F32, name="ident")
        make_identity(nc, ident[:])
        warm = consts.tile([P, 1], F32, name="warm")
        nc.vector.memset(warm[:], 0.0)
        nc.scalar.activation(out=warm[:], in_=warm[:], func=ACT.Sin)

        y_t = {}
        g_t = {}
        d_t = {}
        raw_t = {}
        e4_grouped = {}
        e4_q = {}
        a_q = {}
        b_q = {}
        acc = {}
        grouped_a = {}
        grouped_b = {}
        tp_t = {}

        def rows_of(i):
            return slice(i * PASS, (i + 1) * PASS)

        def load_y(n):
            col, tok = divmod(n, n_tok)
            yt = ypool.tile([P, PACK, PASS], F32, name="yt")
            nc.sync.dma_start(out=yt[:], in_=y[rows_of(tok), rows_of(col)].rearrange("(p j) n -> p j n", j=PACK))
            y_t[n] = yt

        def load_g(n):
            col, tok = divmod(n, n_tok)
            gt = gpool.tile([P, PACK, PASS], BF16, name="gt", align_bytes=64)
            nc.sync.dma_start(out=gt[:], in_=grad_out[rows_of(tok), rows_of(col)].rearrange("(p j) n -> p j n", j=PACK))
            g_t[n] = gt

        def load_e4(label, src, i):
            raw = rawp.tile([P, PACK, IN_F], BF16, name="raw")
            nc.sync.dma_start(out=raw[:], in_=src[rows_of(i), :].rearrange("(p j) k -> p j k", j=PACK))
            raw_t[label] = raw

        def interleave_e4(label):
            grouped = stage.tile([P, IN_F, PACK], BF16, name="grouped_e4", align_bytes=64)
            nc.vector.tensor_copy(out=grouped[:], in_=raw_t[label][:].rearrange("p j k -> p k j"))
            e4_grouped[label] = grouped

        def quantize_e4(label):
            codes = keep.tile([P, IN_F], U32, name="codes_%s" % label, align_bytes=64)
            scales = keep.tile([P, IN_F], U8, name="scales_%s" % label, align_bytes=64)
            nc.vector.quantize_mx(out=codes[:].bitcast(E4), scales=scales[:], in_=e4_grouped[label][:].rearrange("p k j -> p (k j)"))
            e4_q[label] = (codes, scales)

        def absy(n):
            d = dpool.tile([P, 3, PACK, P], F32, name="d")
            yi = y_t[n][:].bitcast(I32).rearrange("p j (q m) -> p (j q) m", m=4)
            nc.vector.tensor_scalar(out=d[:, 1:3, :, :].bitcast(I32).rearrange("p m j q -> p (j q) m"), in0=yi[:, :, 2:4], scalar1=0x7FFFFFFF, scalar2=None, op0=ALU.bitwise_and)
            d_t[n] = d

        def trig3(n):
            d = d_t[n]
            nc.scalar.activation(out=d[:, 2, :, :], in_=d[:, 2, :, :], func=ACT.Sin, scale=-2.0, bias=HALF_PI)
            nc.scalar.activation(out=d[:, 2, :, :], in_=d[:, 2, :, :], func=ACT.Square, scale=0.5, bias=0.5)

        def trig12(n):
            yc = y_t[n][:].rearrange("p j (q m) -> p j q m", m=4)
            d = d_t[n]
            nc.scalar.activation(out=d[:, 1, :, :], in_=d[:, 1, :, :], func=ACT.Sin, scale=-1.0, bias=HALF_PI)
            nc.scalar.activation(out=d[:, 0, :, :], in_=yc[:, :, :, 1], func=ACT.Sin, scale=-1.0)

        def trig(n):
            trig3(n)
            trig12(n)

        def rsq(n):
            d = d_t[n]
            nc.scalar.activation(out=d[:, 2, :, :], in_=d[:, 2, :, :], func=ACT.Abs_reciprocal_sqrt)

        def mult(n):
            gv = g_t[n][:].rearrange("p j (q m) -> p (j q) m", m=4)
            nc.vector.tensor_tensor(out=gv[:, :, 1:4], in0=gv[:, :, 1:4], in1=d_t[n][:].rearrange("p m j q -> p (j q) m"), op=ALU.mult)

        def ia(n):
            ga = stage.tile([P, PASS, PACK], BF16, name="ga", align_bytes=64)
            nc.vector.tensor_copy(out=ga[:], in_=g_t[n][:].rearrange("p j n -> p n j"))
            grouped_a[n] = ga

        def qa(n):
            codes = acodes.tile([P, PASS], U32, name="a_codes", align_bytes=64)
            scales = acodes.tile([P, PASS], U8, name="a_scales", align_bytes=64)
            nc.vector.quantize_mx(out=codes[:].bitcast(E5), scales=scales[:], in_=grouped_a[n][:].rearrange("p n j -> p (n j)"))
            a_q[n] = (codes, scales)

        def ma(n):
            col, tok = divmod(n, n_tok)
            codes, scales = a_q[n]
            xc, xs = e4_q["x%d" % tok]
            for i in range(PASS // P):
                if tok == 0:
                    at = accp.tile([P, IN_F], F32, name="acc%d" % i)
                    acc[i] = at
                cols = slice(i * P, (i + 1) * P)
                nc.tensor.matmul_mx(
                    out=acc[i][:],
                    lhsT=codes[:, cols].bitcast(E5),
                    lhsT_scale=scales[:, cols],
                    rhs=xc[:].bitcast(E4),
                    rhs_scale=xs[:],
                    start=(tok == 0),
                    stop=(tok == n_tok - 1),
                )

        def tp(n):
            words = g_t[n][:].rearrange("p j n -> p (j n)").bitcast(F32)
            banks = []
            for b in range(2):
                bank = wkp.tile([P, 2, 2, P], F32, name="bank", tag="wk")
                for jj in range(2):
                    j = 2 * b + jj
                    for u in range(2):
                        nc.tensor.transpose(bank[:, jj, u, :], words[:, j * 256 + u : (j + 1) * 256 : 2], ident[:])
                banks.append(bank)
            tp_t[n] = banks

        def cb_bank(n, b, on_vector):
            if b == 0:
                gb = stage.tile([P, PACK, P, PACK], BF16, name="gb", align_bytes=64, bufs=5)
                grouped_b[n] = gb
            gbw = grouped_b[n][:].bitcast(F32)
            if on_vector:
                nc.vector.tensor_copy(out=gbw[:, 2 * b : 2 * b + 2, :, :], in_=tp_t[n][b][:].rearrange("p j u r -> p j r u"))
            else:
                nc.scalar.copy(out=gbw[:, 2 * b : 2 * b + 2, :, :], in_=tp_t[n][b][:].rearrange("p j u r -> p j r u"))

        def cb(n):
            cb_bank(n, 0, False)
            cb_bank(n, 1, False)

        def qb(n):
            codes = keep.tile([P, PASS], U32, name="b_codes%d" % n, align_bytes=64)
            scales = keep.tile([P, PASS], U8, name="b_scales%d" % n, align_bytes=64)
            nc.vector.quantize_mx(out=codes[:].bitcast(E5), scales=scales[:], in_=grouped_b[n][:].rearrange("p j r t -> p (j r t)"))
            b_q[n] = (codes, scales)

        def mb_ox(tok):
            dxo = outp.tile([P, PACK, IN_F], F32, name="dxo")
            dst = out_0[rows_of(tok), :].rearrange("(r j) k -> r j k", j=PACK)
            for j in range(PACK):
                ps = wkp.tile([P, IN_F], F32, name="ps", tag="wk")
                cols = slice(j * P, (j + 1) * P)
                for col in range(n_col):
                    codes, scales = b_q[col * n_tok + tok]
                    wc, ws = e4_q["w%d" % col]
                    nc.tensor.matmul_mx(
                        out=ps[:],
                        lhsT=codes[:, cols].bitcast(E5),
                        lhsT_scale=scales[:, cols],
                        rhs=wc[:].bitcast(E4),
                        rhs_scale=ws[:],
                        start=(col == 0),
                        stop=(col == n_col - 1),
                    )
                nc.scalar.copy(out=dxo[:, j, :], in_=ps[:])
                nc.sync.dma_start(out=dst[:, j, :], in_=dxo[:, j, :])

        def ow(col, last):
            dwo = outp.tile([P, PASS // P, IN_F], F32, name="dwo", bufs=1)
            dst = out_1[rows_of(col), :].rearrange("(i p) k -> p i k", p=P)
            for i in range(PASS // P):
                if last and i % 2 == 1:
                    nc.vector.tensor_copy(out=dwo[:, i, :], in_=acc[i][:])
                else:
                    nc.scalar.copy(out=dwo[:, i, :], in_=acc[i][:])
                if last:
                    nc.sync.dma_start(out=dst[:, i, :], in_=dwo[:, i, :])
            if not last:
                nc.sync.dma_start(out=dst, in_=dwo[:])

        load_y(0)
        load_e4("x0", x, 0)
        load_y(1)
        load_e4("x1", x, 1)
        load_y(2)
        load_e4("x2", x, 2)
        load_y(3)

        absy(0)
        trig(0)
        interleave_e4("x0")
        load_e4("x3", x, 3)

        absy(1)
        trig(1)
        quantize_e4("x0")
        interleave_e4("x1")
        load_e4("w0", weight, 0)

        absy(2)
        trig(2)
        quantize_e4("x1")
        interleave_e4("x2")
        load_e4("w1", weight, 1)
        load_g(0)
        load_y(4)
        load_g(1)
        load_y(5)

        absy(3)
        trig3(3)
        quantize_e4("x2")
        interleave_e4("x3")
        load_g(2)
        load_y(6)
        load_y(7)
        load_g(3)
        load_g(4)
        load_g(5)

        for n in range(4):
            rsq(n)
        trig12(3)

        interleave_e4("w0")
        quantize_e4("x3")

        mult(0)
        quantize_e4("w0")
        absy(4)
        tp(0)
        trig(4)
        cb_bank(0, 0, False)
        ia(0)
        load_g(6)

        mult(1)
        absy(5)
        tp(1)
        trig(5)
        cb_bank(0, 1, True)
        cb_bank(1, 0, False)
        qa(0)
        ma(0)
        ia(1)
        load_g(7)

        mult(2)
        absy(6)
        cb_bank(1, 1, True)
        tp(2)
        trig(6)
        qa(1)
        ma(1)
        absy(7)
        ia(2)

        mult(3)
        interleave_e4("w1")
        tp(3)
        trig(7)
        for n in range(4, 8):
            rsq(n)
        qa(2)
        ma(2)
        qb(0)
        ia(3)

        quantize_e4("w1")
        qa(3)
        ma(3)
        cb(2)
        cb(3)

        mult(4)
        tp(4)
        cb(4)
        ow(0, False)
        qb(1)
        ia(4)

        mult(5)
        tp(5)
        cb(5)
        qa(4)
        ma(4)
        qb(4)
        mb_ox(0)

        mult(6)
        tp(6)
        cb(6)
        ia(5)
        qb(5)
        mb_ox(1)
        qb(2)

        mult(7)
        tp(7)
        cb(7)
        qa(5)
        ma(5)
        qb(6)
        mb_ox(2)
        qb(3)
        ia(6)

        qb(7)
        mb_ox(3)
        ia(7)
        qa(6)
        ma(6)
        qa(7)
        ma(7)
        ow(1, True)
